import numpy as np
import ml_dtypes


def mxq(x, axis, fmt="e4m3"):
    dtype, down = {"e4m3": (ml_dtypes.float8_e4m3fn, 7), "e5m2": (ml_dtypes.float8_e5m2, 14)}[fmt]
    v = np.moveaxis(np.asarray(x, np.float32).astype(ml_dtypes.bfloat16).astype(np.float64), axis, -1)
    blocks = v.reshape(v.shape[:-1] + (-1, 32))
    amax = np.abs(blocks).max(-1, keepdims=True)
    byte = np.maximum(np.where(amax > 0, np.frexp(amax)[1] - 1 + 127, 0) - down, 1)
    scale = np.exp2(byte - 127.0)
    codes = (blocks / scale).astype(np.float32).astype(dtype).astype(np.float64)
    return np.moveaxis((codes * scale).reshape(v.shape), -1, axis)


WIDE = False


def mx_kscale(k):
    if not WIDE:
        return np.ones(k)
    levels = np.array([10, -10, 5, -5, 0])
    a = np.random.permutation(np.resize(levels, k // 512 * 4)).reshape(k // 512, 4)
    idx = np.arange(k)
    return np.exp2(a[idx // 512, idx % 128 // 32])


BF16 = ml_dtypes.bfloat16


def bf(x):
    return np.asarray(x, np.float32).astype(BF16)


def f64(x):
    return np.asarray(x).astype(np.float64)


B, H, W, C, NF, ZD = 128, 4, 4, 8192, 128, 512
EPS = 1e-8
LRELU_SLOPE = 0.2


def setup_inputs():
    s = mx_kscale(C)
    return {"x": bf(np.random.standard_normal((B, H, W, C)) * s),
            "dlatents": bf(np.random.standard_normal((B, ZD))),
            "noise_map": bf(np.random.standard_normal((B, H, W, 1))),
            "conv_w": bf(np.random.standard_normal((C, NF)) / np.sqrt(C) / s[:, None]),
            "noise_weight": bf(np.random.standard_normal((1, 1, 1, NF)) * 0.5),
            "bias": bf(np.random.standard_normal((1, 1, 1, NF)) * 0.5),
            "dense_w": bf(np.random.standard_normal((ZD, 2 * NF)) / np.sqrt(ZD)),
            "dense_b": bf(np.random.standard_normal(2 * NF) * 0.3)}


def reference(x, dlatents, noise_map, conv_w, noise_weight, bias, dense_w, dense_b):
    y = mxq(f64(x), 3, "e4m3") @ mxq(f64(conv_w), 0, "e4m3")
    y = y + f64(noise_weight) * f64(noise_map) + f64(bias)
    y = np.where(y >= 0.0, y, LRELU_SLOPE * y)
    mu = np.mean(y, axis=(1, 2), keepdims=True)
    var = np.mean(np.square(y - mu), axis=(1, 2), keepdims=True)
    yn = (y - mu) / np.sqrt(var + EPS)
    gb = f64(dlatents) @ f64(dense_w) + f64(dense_b)
    nf = y.shape[-1]
    gb = gb.reshape(-1, 2, 1, 1, nf)
    gamma, beta = gb[:, 0], gb[:, 1]
    return yn * (1.0 + gamma) + beta

@@ -1,0 +1,341 @@
+from contextlib import ExitStack
+
+import concourse.mybir as mybir
+from concourse.masks import make_identity
+
+F32 = mybir.dt.float32
+BF16 = mybir.dt.bfloat16
+U32 = mybir.dt.uint32
+U8 = mybir.dt.uint8
+FP8X4 = mybir.dt.float8_e4m3fn_x4
+ALU = mybir.AluOpType
+ACT = mybir.ActivationFunctionType
+
+P = 128
+PIXELS = 16
+CHANNELS = 8192
+FILTERS = 128
+LATENT = 512
+EPS = 1e-8
+SLOPE = 0.2
+
+PACK = 4
+K_PASS = P * PACK
+PASSES = CHANNELS // K_PASS
+CHUNK_PASSES = 8
+CHUNK_COLS = CHUNK_PASSES * K_PASS
+CHUNKS_PER_PIXEL = PASSES // CHUNK_PASSES
+N_CHUNKS = PIXELS * CHUNKS_PER_PIXEL
+BANK_PASSES = 2
+BANKS_PER_CHUNK = CHUNK_PASSES // BANK_PASSES
+QUANT_PASSES = 8
+W_PIECES = 4
+W_PIECE_PASSES = PASSES // W_PIECES
+X_BUFS = 6
+
+FLOPS = 2 * P * PIXELS * CHANNELS * FILTERS + 2 * P * LATENT * 2 * FILTERS
+
+
+def tile_styleganlayerepilogue_k_kernel(
+    tc, x, dlatents, noise_map, conv_w, noise_weight, bias, dense_w, dense_b, out
+):
+    nc = tc.nc
+    x_rows = x.rearrange("b h w c -> b (h w) c")
+    out_rows = out.rearrange("b h w n -> b (h w) n")
+
+    with ExitStack() as ctx:
+        ctx.enter_context(tc.manual_schedule())
+        keep = ctx.enter_context(tc.tile_pool(name="keep", bufs=1))
+        x_pool = ctx.enter_context(tc.tile_pool(name="x_pool", bufs=X_BUFS))
+        grouped_pool = ctx.enter_context(tc.tile_pool(name="grouped_pool", bufs=3))
+        codes_pool = ctx.enter_context(tc.tile_pool(name="codes_pool", bufs=3))
+        work = ctx.enter_context(tc.tile_pool(name="work", bufs=3))
+        banks = ctx.enter_context(tc.psum_pool(name="banks", bufs=6))
+        sums = ctx.enter_context(tc.psum_pool(name="sums", bufs=2))
+
+        x_chunks = {}
+        grouped_tiles = {}
+        code_tiles = {}
+        scale_tiles = {}
+        conv_sums = {}
+        pre_relu = {}
+        squares = {}
+
+        latents = keep.tile([P, LATENT], BF16)
+        nc.scalar.dma_start(out=latents[:], in_=dlatents)
+        dense = keep.tile([P, LATENT // P, 2 * FILTERS], BF16)
+        nc.scalar.dma_start(out=dense[:], in_=dense_w.rearrange("(c p) n -> p c n", p=P))
+        noise_bf = keep.tile([P, PIXELS], BF16)
+        nc.scalar.dma_start(out=noise_bf[:], in_=noise_map.rearrange("b h w o -> b (h w o)"))
+        rows = keep.tile([P, 4 * FILTERS], BF16)
+        nc.vector.memset(rows[:], 0.0)
+        nc.scalar.dma_start(
+            out=rows[0:1, 0:FILTERS], in_=noise_weight.rearrange("a b c n -> (a b c) n")
+        )
+        nc.scalar.dma_start(
+            out=rows[0:1, FILTERS : 2 * FILTERS], in_=bias.rearrange("a b c n -> (a b c) n")
+        )
+        nc.scalar.dma_start(
+            out=rows[0:1, 2 * FILTERS : 4 * FILTERS], in_=dense_b.rearrange("(o n) -> o n", o=1)
+        )
+
+        w_raw = keep.tile([P, PASSES, PACK, FILTERS], BF16)
+        w_view = conv_w.rearrange("(s p e) n -> p s (e n)", p=P, e=2)
+        for piece in range(W_PIECES):
+            passes = slice(piece * W_PIECE_PASSES, (piece + 1) * W_PIECE_PASSES)
+            halves = slice(piece * W_PIECE_PASSES * 2, (piece + 1) * W_PIECE_PASSES * 2)
+            nc.sync.dma_start(
+                out=w_raw[:, passes, :, :].rearrange("p c (u e) n -> p (c u) (e n)", u=2),
+                in_=w_view[:, halves, :],
+            )
+
+        def load(i):
+            if i >= N_CHUNKS:
+                return
+            pixel, part = divmod(i, CHUNKS_PER_PIXEL)
+            x_chunk = x_pool.tile([P, CHUNK_COLS], BF16, name="x_chunk")
+            nc.sync.dma_start(
+                out=x_chunk[:], in_=x_rows[:, pixel, part * CHUNK_COLS : (part + 1) * CHUNK_COLS]
+            )
+            x_chunks[i] = x_chunk
+
+        for i in range(X_BUFS):
+            load(i)
+
+        ident_f32 = keep.tile([P, P], F32)
+        make_identity(nc, ident_f32[:])
+        ident_bf = keep.tile([P, P], BF16)
+        make_identity(nc, ident_bf[:])
+        ones = keep.tile([P, P], BF16)
+        nc.vector.memset(ones[:], 1.0)
+        dev_sum = keep.tile([P, FILTERS], F32)
+        nc.vector.memset(dev_sum[:], 0.0)
+        sq_sum = keep.tile([P, FILTERS], F32)
+        nc.vector.memset(sq_sum[:], 0.0)
+        one = keep.tile([P, 1], F32)
+        nc.vector.memset(one[:], 1.0)
+        warm = keep.tile([P, 1], F32)
+        nc.scalar.activation(out=warm[:], in_=one[:], func=ACT.Sqrt)
+
+        latents_t_ps = banks.tile([P, LATENT // P, P], BF16, tag="bank")
+        for c in range(LATENT // P):
+            nc.tensor.transpose(latents_t_ps[:, c, :], latents[:, c * P : (c + 1) * P], ident_bf[:])
+        latents_t = keep.tile([P, LATENT // P, P], BF16)
+        nc.vector.tensor_copy(out=latents_t[:], in_=latents_t_ps[:])
+
+        spread_ps = banks.tile([P, 4 * FILTERS], F32, tag="bank")
+        nc.tensor.matmul(
+            out=spread_ps[:, 0 : 2 * FILTERS],
+            lhsT=ones[:],
+            rhs=rows[:, 0 : 2 * FILTERS],
+            start=True,
+            stop=True,
+        )
+        for c in range(LATENT // P):
+            nc.tensor.matmul(
+                out=spread_ps[:, 2 * FILTERS : 4 * FILTERS],
+                lhsT=latents_t[:, c, :],
+                rhs=dense[:, c, :],
+                start=(c == 0),
+                stop=False,
+            )
+        nc.tensor.matmul(
+            out=spread_ps[:, 2 * FILTERS : 4 * FILTERS],
+            lhsT=ones[:],
+            rhs=rows[:, 2 * FILTERS : 4 * FILTERS],
+            start=False,
+            stop=True,
+        )
+        per_channel = keep.tile([P, 2 * FILTERS], F32)
+        nc.vector.tensor_copy(out=per_channel[:], in_=spread_ps[:, 0 : 2 * FILTERS])
+        gamma1 = keep.tile([P, FILTERS], F32)
+        nc.vector.tensor_scalar_add(
+            out=gamma1[:], in0=spread_ps[:, 2 * FILTERS : 3 * FILTERS], scalar1=1.0
+        )
+        beta = keep.tile([P, FILTERS], F32)
+        nc.vector.tensor_copy(out=beta[:], in_=spread_ps[:, 3 * FILTERS : 4 * FILTERS])
+
+        noise = keep.tile([P, PIXELS], F32)
+        nc.vector.tensor_copy(out=noise[:], in_=noise_bf[:])
+        noise_bias = keep.tile([P, PIXELS, FILTERS], F32)
+        for pixel in range(PIXELS):
+            nc.vector.scalar_tensor_tensor(
+                out=noise_bias[:, pixel, :],
+                in0=per_channel[:, 0:FILTERS],
+                scalar=noise[:, pixel : pixel + 1],
+                in1=per_channel[:, FILTERS : 2 * FILTERS],
+                op0=ALU.mult,
+                op1=ALU.add,
+            )
+
+        w_grouped = keep.tile([P, PASSES, FILTERS, PACK], BF16, align_bytes=64)
+        w_codes = keep.tile([P, PASSES * FILTERS], U32, align_bytes=64)
+        w_scales = keep.tile([P, PASSES * FILTERS], U8, align_bytes=64)
+        for piece in range(W_PIECES):
+            passes = slice(piece * W_PIECE_PASSES, (piece + 1) * W_PIECE_PASSES)
+            regroup = nc.scalar.copy if piece % 2 == 0 else nc.vector.tensor_copy
+            regroup(
+                out=w_grouped[:, passes, :, :],
+                in_=w_raw[:, passes, :, :].rearrange("p c t n -> p c n t"),
+            )
+        for piece in range(W_PIECES):
+            passes = slice(piece * W_PIECE_PASSES, (piece + 1) * W_PIECE_PASSES)
+            cols = slice(piece * W_PIECE_PASSES * FILTERS, (piece + 1) * W_PIECE_PASSES * FILTERS)
+            nc.vector.quantize_mx(
+                out=w_codes[:, cols].bitcast(FP8X4),
+                scales=w_scales[:, cols],
+                in_=w_grouped[:, passes, :, :].rearrange("p c n t -> p (c n t)"),
+            )
+
+        def transpose(i):
+            if i >= N_CHUNKS:
+                return
+            words = x_chunks[i][:].bitcast(F32)
+            grouped = grouped_pool.tile([P, CHUNK_COLS], BF16, align_bytes=64, name="grouped")
+            grouped_words = grouped[:].bitcast(F32).rearrange("p (g r u) -> p g r u", r=P, u=2)
+            for bank in range(BANKS_PER_CHUNK):
+                xt = banks.tile([P, BANK_PASSES, 2, P], F32, tag="bank", name="xt")
+                for g in range(BANK_PASSES):
+                    for u in range(2):
+                        first = ((bank * BANK_PASSES + g) * 2 + u) * P
+                        nc.tensor.transpose(xt[:, g, u, :], words[:, first : first + P], ident_f32[:])
+                empty = nc.vector.tensor_copy if bank == BANKS_PER_CHUNK - 1 else nc.scalar.copy
+                empty(
+                    out=grouped_words[:, bank * BANK_PASSES : (bank + 1) * BANK_PASSES, :, :],
+                    in_=xt[:].rearrange("p g u r -> p g r u"),
+                )
+            grouped_tiles[i] = grouped
+
+        def quantise(i):
+            if i < 0 or i >= N_CHUNKS:
+                return
+            codes = codes_pool.tile([P, CHUNK_PASSES * P], U32, align_bytes=64, name="codes")
+            scales = codes_pool.tile([P, CHUNK_PASSES * P], U8, align_bytes=64, name="scales")
+            for first in range(0, CHUNK_PASSES, QUANT_PASSES):
+                cols = slice(first * P, (first + QUANT_PASSES) * P)
+                values = slice(first * P * PACK, (first + QUANT_PASSES) * P * PACK)
+                nc.vector.quantize_mx(
+                    out=codes[:, cols].bitcast(FP8X4),
+                    scales=scales[:, cols],
+                    in_=grouped_tiles[i][:, values],
+                )
+            code_tiles[i] = codes
+            scale_tiles[i] = scales
+
+        def multiply(i):
+            if i < 0 or i >= N_CHUNKS:
+                return
+            pixel, part = divmod(i, CHUNKS_PER_PIXEL)
+            if part == 0:
+                conv_sums[pixel] = sums.tile([P, FILTERS], F32, name="conv_sum")
+            for g in range(CHUNK_PASSES):
+                c = part * CHUNK_PASSES + g
+                nc.tensor.matmul_mx(
+                    out=conv_sums[pixel][:],
+                    lhsT=code_tiles[i][:, g * P : (g + 1) * P].bitcast(FP8X4),
+                    lhsT_scale=scale_tiles[i][:, g * P : (g + 1) * P],
+                    rhs=w_codes[:, c * FILTERS : (c + 1) * FILTERS].bitcast(FP8X4),
+                    rhs_scale=w_scales[:, c * FILTERS : (c + 1) * FILTERS],
+                    start=(c == 0),
+                    stop=(c == PASSES - 1),
+                )
+
+        def closes_pixel(i):
+            return 0 <= i < N_CHUNKS and i % CHUNKS_PER_PIXEL == CHUNKS_PER_PIXEL - 1
+
+        relu = keep.tile([P, PIXELS, FILTERS], F32)
+        dev = keep.tile([P, PIXELS, FILTERS], F32)
+
+        def add_noise(i):
+            if not closes_pixel(i):
+                return
+            pixel = i // CHUNKS_PER_PIXEL
+            pre_relu[pixel] = work.tile([P, FILTERS], F32, name="pre")
+            nc.vector.tensor_tensor(
+                out=pre_relu[pixel][:],
+                in0=conv_sums[pixel][:],
+                in1=noise_bias[:, pixel, :],
+                op=ALU.add,
+            )
+
+        def leaky_relu(i):
+            if not closes_pixel(i):
+                return
+            pixel = i // CHUNKS_PER_PIXEL
+            nc.vector.scalar_tensor_tensor(
+                out=relu[:, pixel, :],
+                in0=pre_relu[pixel][:],
+                scalar=SLOPE,
+                in1=pre_relu[pixel][:],
+                op0=ALU.mult,
+                op1=ALU.max,
+            )
+            nc.gpsimd.tensor_tensor(
+                out=dev[:, pixel, :], in0=relu[:, pixel, :], in1=relu[:, 0, :], op=ALU.subtract
+            )
+            nc.gpsimd.tensor_tensor(
+                out=dev_sum[:], in0=dev_sum[:], in1=dev[:, pixel, :], op=ALU.add
+            )
+
+        def square(i):
+            if not closes_pixel(i):
+                return
+            pixel = i // CHUNKS_PER_PIXEL
+            squares[pixel] = work.tile([P, FILTERS], F32, name="sq")
+            nc.scalar.activation(out=squares[pixel][:], in_=dev[:, pixel, :], func=ACT.Square)
+            nc.gpsimd.tensor_tensor(out=sq_sum[:], in0=sq_sum[:], in1=squares[pixel][:], op=ALU.add)
+
+        for step in range(N_CHUNKS + 3):
+            add_noise(step - 3)
+            quantise(step - 1)
+            leaky_relu(step - 3)
+            transpose(step)
+            load(step + X_BUFS)
+            multiply(step - 2)
+            square(step - 3)
+
+        mean = keep.tile([P, FILTERS], F32)
+        nc.vector.tensor_scalar_mul(out=mean[:], in0=dev_sum[:], scalar1=1.0 / PIXELS)
+        mean_sq = keep.tile([P, FILTERS], F32)
+        nc.vector.tensor_mul(out=mean_sq[:], in0=mean[:], in1=mean[:])
+        second = keep.tile([P, FILTERS], F32)
+        nc.vector.tensor_scalar(
+            out=second[:],
+            in0=sq_sum[:],
+            scalar1=1.0 / PIXELS,
+            scalar2=EPS,
+            op0=ALU.mult,
+            op1=ALU.add,
+        )
+        var_eps = keep.tile([P, FILTERS], F32)
+        nc.vector.tensor_sub(out=var_eps[:], in0=second[:], in1=mean_sq[:])
+        std = keep.tile([P, FILTERS], F32)
+        nc.scalar.activation(out=std[:], in_=var_eps[:], func=ACT.Sqrt)
+        inv_std = keep.tile([P, FILTERS], F32)
+        nc.vector.reciprocal(out=inv_std[:], in_=std[:])
+        gain = keep.tile([P, FILTERS], F32)
+        nc.vector.tensor_mul(out=gain[:], in0=inv_std[:], in1=gamma1[:])
+        mean_gain = keep.tile([P, FILTERS], F32)
+        nc.vector.tensor_mul(out=mean_gain[:], in0=mean[:], in1=gain[:])
+        shift = keep.tile([P, FILTERS], F32)
+        nc.vector.tensor_sub(out=shift[:], in0=beta[:], in1=mean_gain[:])
+
+        result = keep.tile([P, PIXELS, FILTERS], F32)
+        STORE_PIXELS = 4
+        for first in range(0, PIXELS, STORE_PIXELS):
+            some = slice(first, first + STORE_PIXELS)
+            nc.vector.tensor_tensor(
+                out=result[:, some, :],
+                in0=dev[:, some, :],
+                in1=gain[:].unsqueeze(1).to_broadcast([P, STORE_PIXELS, FILTERS]),
+                op=ALU.mult,
+            )
+        for first in range(0, PIXELS, STORE_PIXELS):
+            some = slice(first, first + STORE_PIXELS)
+            nc.vector.tensor_tensor(
+                out=result[:, some, :],
+                in0=result[:, some, :],
+                in1=shift[:].unsqueeze(1).to_broadcast([P, STORE_PIXELS, FILTERS]),
+                op=ALU.add,
+            )
+            nc.sync.dma_start(out=out_rows[:, some, :], in_=result[:, some, :])

@@ -24,16 +24,27 @@ K_PASS = P * PACK
 PASSES = CHANNELS // K_PASS
 CHUNK_PASSES = 8
 CHUNK_COLS = CHUNK_PASSES * K_PASS
-CHUNKS_PER_PIXEL = PASSES // CHUNK_PASSES
-N_CHUNKS = PIXELS * CHUNKS_PER_PIXEL
 BANK_PASSES = 2
-BANKS_PER_CHUNK = CHUNK_PASSES // BANK_PASSES
-QUANT_PASSES = 8
 W_PIECES = 4
 W_PIECE_PASSES = PASSES // W_PIECES
 X_BUFS = 6
 
 FLOPS = 2 * P * PIXELS * CHANNELS * FILTERS + 2 * P * LATENT * 2 * FILTERS
+
+
+def cut_into_chunks():
+    chunks = []
+    for pixel in range(PIXELS):
+        for first in range(0, PASSES, CHUNK_PASSES):
+            chunks.append((pixel, first, CHUNK_PASSES))
+    pixel, first, left = chunks[-1]
+    chunks = chunks[:-1]
+    while left > BANK_PASSES:
+        chunks.append((pixel, first, left // 2))
+        first += left // 2
+        left -= left // 2
+    chunks.append((pixel, first, left))
+    return chunks
 
 
 def tile_styleganlayerepilogue_k_kernel(
@@ -42,13 +53,15 @@ def tile_styleganlayerepilogue_k_kernel(
     nc = tc.nc
     x_rows = x.rearrange("b h w c -> b (h w) c")
     out_rows = out.rearrange("b h w n -> b (h w) n")
+    chunks = cut_into_chunks()
+    n_chunks = len(chunks)
 
     with ExitStack() as ctx:
         ctx.enter_context(tc.manual_schedule())
         keep = ctx.enter_context(tc.tile_pool(name="keep", bufs=1))
         x_pool = ctx.enter_context(tc.tile_pool(name="x_pool", bufs=X_BUFS))
         grouped_pool = ctx.enter_context(tc.tile_pool(name="grouped_pool", bufs=3))
-        codes_pool = ctx.enter_context(tc.tile_pool(name="codes_pool", bufs=3))
+        codes_pool = ctx.enter_context(tc.tile_pool(name="codes_pool", bufs=4))
         work = ctx.enter_context(tc.tile_pool(name="work", bufs=3))
         banks = ctx.enter_context(tc.psum_pool(name="banks", bufs=6))
         sums = ctx.enter_context(tc.psum_pool(name="sums", bufs=2))
@@ -90,12 +103,13 @@ def tile_styleganlayerepilogue_k_kernel(
             )
 
         def load(i):
-            if i >= N_CHUNKS:
+            if i >= n_chunks:
                 return
-            pixel, part = divmod(i, CHUNKS_PER_PIXEL)
+            pixel, first, passes = chunks[i]
             x_chunk = x_pool.tile([P, CHUNK_COLS], BF16, name="x_chunk")
             nc.sync.dma_start(
-                out=x_chunk[:], in_=x_rows[:, pixel, part * CHUNK_COLS : (part + 1) * CHUNK_COLS]
+                out=x_chunk[:, : passes * K_PASS],
+                in_=x_rows[:, pixel, first * K_PASS : (first + passes) * K_PASS],
             )
             x_chunks[i] = x_chunk
 
@@ -111,11 +125,11 @@ def tile_styleganlayerepilogue_k_kernel(
         dev_sum = keep.tile([P, FILTERS], F32)
         nc.vector.memset(dev_sum[:], 0.0)
         sq_sum = keep.tile([P, FILTERS], F32)
-        nc.vector.memset(sq_sum[:], 0.0)
+        nc.vector.memset(sq_sum[:], PIXELS * EPS)
         one = keep.tile([P, 1], F32)
         nc.vector.memset(one[:], 1.0)
         warm = keep.tile([P, 1], F32)
-        nc.scalar.activation(out=warm[:], in_=one[:], func=ACT.Sqrt)
+        nc.scalar.activation(out=warm[:], in_=one[:], func=ACT.Abs_reciprocal_sqrt)
 
         latents_t_ps = banks.tile([P, LATENT // P, P], BF16, tag="bank")
         for c in range(LATENT // P):
@@ -188,18 +202,19 @@ def tile_styleganlayerepilogue_k_kernel(
             )
 
         def transpose(i):
-            if i >= N_CHUNKS:
+            if i >= n_chunks:
                 return
+            passes = chunks[i][2]
             words = x_chunks[i][:].bitcast(F32)
             grouped = grouped_pool.tile([P, CHUNK_COLS], BF16, align_bytes=64, name="grouped")
             grouped_words = grouped[:].bitcast(F32).rearrange("p (g r u) -> p g r u", r=P, u=2)
-            for bank in range(BANKS_PER_CHUNK):
+            for bank in range(passes // BANK_PASSES):
                 xt = banks.tile([P, BANK_PASSES, 2, P], F32, tag="bank", name="xt")
                 for g in range(BANK_PASSES):
                     for u in range(2):
                         first = ((bank * BANK_PASSES + g) * 2 + u) * P
                         nc.tensor.transpose(xt[:, g, u, :], words[:, first : first + P], ident_f32[:])
-                empty = nc.vector.tensor_copy if bank == BANKS_PER_CHUNK - 1 else nc.scalar.copy
+                empty = nc.vector.tensor_copy if bank == 3 else nc.scalar.copy
                 empty(
                     out=grouped_words[:, bank * BANK_PASSES : (bank + 1) * BANK_PASSES, :, :],
                     in_=xt[:].rearrange("p g u r -> p g r u"),
@@ -207,29 +222,27 @@ def tile_styleganlayerepilogue_k_kernel(
             grouped_tiles[i] = grouped
 
         def quantise(i):
-            if i < 0 or i >= N_CHUNKS:
+            if i < 0 or i >= n_chunks:
                 return
+            passes = chunks[i][2]
             codes = codes_pool.tile([P, CHUNK_PASSES * P], U32, align_bytes=64, name="codes")
             scales = codes_pool.tile([P, CHUNK_PASSES * P], U8, align_bytes=64, name="scales")
-            for first in range(0, CHUNK_PASSES, QUANT_PASSES):
-                cols = slice(first * P, (first + QUANT_PASSES) * P)
-                values = slice(first * P * PACK, (first + QUANT_PASSES) * P * PACK)
-                nc.vector.quantize_mx(
-                    out=codes[:, cols].bitcast(FP8X4),
-                    scales=scales[:, cols],
-                    in_=grouped_tiles[i][:, values],
-                )
+            nc.vector.quantize_mx(
+                out=codes[:, : passes * P].bitcast(FP8X4),
+                scales=scales[:, : passes * P],
+                in_=grouped_tiles[i][:, : passes * K_PASS],
+            )
             code_tiles[i] = codes
             scale_tiles[i] = scales
 
         def multiply(i):
-            if i < 0 or i >= N_CHUNKS:
+            if i < 0 or i >= n_chunks:
                 return
-            pixel, part = divmod(i, CHUNKS_PER_PIXEL)
-            if part == 0:
+            pixel, first, passes = chunks[i]
+            if first == 0:
                 conv_sums[pixel] = sums.tile([P, FILTERS], F32, name="conv_sum")
-            for g in range(CHUNK_PASSES):
-                c = part * CHUNK_PASSES + g
+            for g in range(passes):
+                c = first + g
                 nc.tensor.matmul_mx(
                     out=conv_sums[pixel][:],
                     lhsT=code_tiles[i][:, g * P : (g + 1) * P].bitcast(FP8X4),
@@ -241,7 +254,7 @@ def tile_styleganlayerepilogue_k_kernel(
                 )
 
         def closes_pixel(i):
-            return 0 <= i < N_CHUNKS and i % CHUNKS_PER_PIXEL == CHUNKS_PER_PIXEL - 1
+            return 0 <= i < n_chunks and chunks[i][1] + chunks[i][2] == PASSES
 
         relu = keep.tile([P, PIXELS, FILTERS], F32)
         dev = keep.tile([P, PIXELS, FILTERS], F32)
@@ -249,7 +262,7 @@ def tile_styleganlayerepilogue_k_kernel(
         def add_noise(i):
             if not closes_pixel(i):
                 return
-            pixel = i // CHUNKS_PER_PIXEL
+            pixel = chunks[i][0]
             pre_relu[pixel] = work.tile([P, FILTERS], F32, name="pre")
             nc.vector.tensor_tensor(
                 out=pre_relu[pixel][:],
@@ -261,7 +274,7 @@ def tile_styleganlayerepilogue_k_kernel(
         def leaky_relu(i):
             if not closes_pixel(i):
                 return
-            pixel = i // CHUNKS_PER_PIXEL
+            pixel = chunks[i][0]
             nc.vector.scalar_tensor_tensor(
                 out=relu[:, pixel, :],
                 in0=pre_relu[pixel][:],
@@ -280,45 +293,44 @@ def tile_styleganlayerepilogue_k_kernel(
         def square(i):
             if not closes_pixel(i):
                 return
-            pixel = i // CHUNKS_PER_PIXEL
+            pixel = chunks[i][0]
             squares[pixel] = work.tile([P, FILTERS], F32, name="sq")
             nc.scalar.activation(out=squares[pixel][:], in_=dev[:, pixel, :], func=ACT.Square)
             nc.gpsimd.tensor_tensor(out=sq_sum[:], in0=sq_sum[:], in1=squares[pixel][:], op=ALU.add)
 
-        for step in range(N_CHUNKS + 3):
+        for step in range(n_chunks + 3):
             add_noise(step - 3)
             quantise(step - 1)
             leaky_relu(step - 3)
             transpose(step)
             load(step + X_BUFS)
-            multiply(step - 2)
+            if step % 2 == 1:
+                multiply(step - 3)
+                multiply(step - 2)
             square(step - 3)
 
-        mean = keep.tile([P, FILTERS], F32)
-        nc.vector.tensor_scalar_mul(out=mean[:], in0=dev_sum[:], scalar1=1.0 / PIXELS)
-        mean_sq = keep.tile([P, FILTERS], F32)
-        nc.vector.tensor_mul(out=mean_sq[:], in0=mean[:], in1=mean[:])
-        second = keep.tile([P, FILTERS], F32)
-        nc.vector.tensor_scalar(
-            out=second[:],
+        minus_mean_sq = keep.tile([P, FILTERS], F32)
+        nc.vector.scalar_tensor_tensor(
+            out=minus_mean_sq[:],
+            in0=dev_sum[:],
+            scalar=-1.0 / (PIXELS * PIXELS),
+            in1=dev_sum[:],
+            op0=ALU.mult,
+            op1=ALU.mult,
+        )
+        var_eps = keep.tile([P, FILTERS], F32)
+        nc.vector.scalar_tensor_tensor(
+            out=var_eps[:],
             in0=sq_sum[:],
-            scalar1=1.0 / PIXELS,
-            scalar2=EPS,
+            scalar=1.0 / PIXELS,
+            in1=minus_mean_sq[:],
             op0=ALU.mult,
             op1=ALU.add,
         )
-        var_eps = keep.tile([P, FILTERS], F32)
-        nc.vector.tensor_sub(out=var_eps[:], in0=second[:], in1=mean_sq[:])
-        std = keep.tile([P, FILTERS], F32)
-        nc.scalar.activation(out=std[:], in_=var_eps[:], func=ACT.Sqrt)
         inv_std = keep.tile([P, FILTERS], F32)
-        nc.vector.reciprocal(out=inv_std[:], in_=std[:])
+        nc.scalar.activation(out=inv_std[:], in_=var_eps[:], func=ACT.Abs_reciprocal_sqrt)
         gain = keep.tile([P, FILTERS], F32)
         nc.vector.tensor_mul(out=gain[:], in0=inv_std[:], in1=gamma1[:])
-        mean_gain = keep.tile([P, FILTERS], F32)
-        nc.vector.tensor_mul(out=mean_gain[:], in0=mean[:], in1=gain[:])
-        shift = keep.tile([P, FILTERS], F32)
-        nc.vector.tensor_sub(out=shift[:], in0=beta[:], in1=mean_gain[:])
 
         result = keep.tile([P, PIXELS, FILTERS], F32)
         STORE_PIXELS = 4
@@ -330,6 +342,17 @@ def tile_styleganlayerepilogue_k_kernel(
                 in1=gain[:].unsqueeze(1).to_broadcast([P, STORE_PIXELS, FILTERS]),
                 op=ALU.mult,
             )
+        mean_gain = keep.tile([P, FILTERS], F32)
+        nc.vector.scalar_tensor_tensor(
+            out=mean_gain[:],
+            in0=dev_sum[:],
+            scalar=1.0 / PIXELS,
+            in1=gain[:],
+            op0=ALU.mult,
+            op1=ALU.mult,
+        )
+        shift = keep.tile([P, FILTERS], F32)
+        nc.vector.tensor_sub(out=shift[:], in0=beta[:], in1=mean_gain[:])
         for first in range(0, PIXELS, STORE_PIXELS):
             some = slice(first, first + STORE_PIXELS)
             nc.vector.tensor_tensor(

from contextlib import ExitStack

import concourse.mybir as mybir
from concourse.masks import make_identity

F32 = mybir.dt.float32
BF16 = mybir.dt.bfloat16
U32 = mybir.dt.uint32
U8 = mybir.dt.uint8
FP8X4 = mybir.dt.float8_e4m3fn_x4
ALU = mybir.AluOpType
ACT = mybir.ActivationFunctionType

P = 128
PIXELS = 16
CHANNELS = 8192
FILTERS = 128
LATENT = 512
EPS = 1e-8
SLOPE = 0.2

PACK = 4
K_PASS = P * PACK
PASSES = CHANNELS // K_PASS
CHUNK_PASSES = 8
CHUNK_COLS = CHUNK_PASSES * K_PASS
BANK_PASSES = 2
W_PIECES = 4
W_PIECE_PASSES = PASSES // W_PIECES
X_BUFS = 6

FLOPS = 2 * P * PIXELS * CHANNELS * FILTERS + 2 * P * LATENT * 2 * FILTERS


def cut_into_chunks():
    chunks = []
    for pixel in range(PIXELS):
        for first in range(0, PASSES, CHUNK_PASSES):
            chunks.append((pixel, first, CHUNK_PASSES))
    pixel, first, left = chunks[-1]
    chunks = chunks[:-1]
    while left > BANK_PASSES:
        chunks.append((pixel, first, left // 2))
        first += left // 2
        left -= left // 2
    chunks.append((pixel, first, left))
    return chunks


def tile_styleganlayerepilogue_k_kernel(
    tc, x, dlatents, noise_map, conv_w, noise_weight, bias, dense_w, dense_b, out
):
    nc = tc.nc
    x_rows = x.rearrange("b h w c -> b (h w) c")
    out_rows = out.rearrange("b h w n -> b (h w) n")
    chunks = cut_into_chunks()
    n_chunks = len(chunks)

    with ExitStack() as ctx:
        ctx.enter_context(tc.manual_schedule())
        keep = ctx.enter_context(tc.tile_pool(name="keep", bufs=1))
        x_pool = ctx.enter_context(tc.tile_pool(name="x_pool", bufs=X_BUFS))
        grouped_pool = ctx.enter_context(tc.tile_pool(name="grouped_pool", bufs=3))
        codes_pool = ctx.enter_context(tc.tile_pool(name="codes_pool", bufs=4))
        work = ctx.enter_context(tc.tile_pool(name="work", bufs=3))
        banks = ctx.enter_context(tc.psum_pool(name="banks", bufs=6))
        sums = ctx.enter_context(tc.psum_pool(name="sums", bufs=2))

        x_chunks = {}
        grouped_tiles = {}
        code_tiles = {}
        scale_tiles = {}
        conv_sums = {}
        pre_relu = {}
        squares = {}

        latents = keep.tile([P, LATENT], BF16)
        nc.scalar.dma_start(out=latents[:], in_=dlatents)
        dense = keep.tile([P, LATENT // P, 2 * FILTERS], BF16)
        nc.scalar.dma_start(out=dense[:], in_=dense_w.rearrange("(c p) n -> p c n", p=P))
        noise_bf = keep.tile([P, PIXELS], BF16)
        nc.scalar.dma_start(out=noise_bf[:], in_=noise_map.rearrange("b h w o -> b (h w o)"))
        rows = keep.tile([P, 4 * FILTERS], BF16)
        nc.vector.memset(rows[:], 0.0)
        nc.scalar.dma_start(
            out=rows[0:1, 0:FILTERS], in_=noise_weight.rearrange("a b c n -> (a b c) n")
        )
        nc.scalar.dma_start(
            out=rows[0:1, FILTERS : 2 * FILTERS], in_=bias.rearrange("a b c n -> (a b c) n")
        )
        nc.scalar.dma_start(
            out=rows[0:1, 2 * FILTERS : 4 * FILTERS], in_=dense_b.rearrange("(o n) -> o n", o=1)
        )

        w_raw = keep.tile([P, PASSES, PACK, FILTERS], BF16)
        w_view = conv_w.rearrange("(s p e) n -> p s (e n)", p=P, e=2)
        for piece in range(W_PIECES):
            passes = slice(piece * W_PIECE_PASSES, (piece + 1) * W_PIECE_PASSES)
            halves = slice(piece * W_PIECE_PASSES * 2, (piece + 1) * W_PIECE_PASSES * 2)
            nc.sync.dma_start(
                out=w_raw[:, passes, :, :].rearrange("p c (u e) n -> p (c u) (e n)", u=2),
                in_=w_view[:, halves, :],
            )

        def load(i):
            if i >= n_chunks:
                return
            pixel, first, passes = chunks[i]
            x_chunk = x_pool.tile([P, CHUNK_COLS], BF16, name="x_chunk")
            nc.sync.dma_start(
                out=x_chunk[:, : passes * K_PASS],
                in_=x_rows[:, pixel, first * K_PASS : (first + passes) * K_PASS],
            )
            x_chunks[i] = x_chunk

        for i in range(X_BUFS):
            load(i)

        ident_f32 = keep.tile([P, P], F32)
        make_identity(nc, ident_f32[:])
        ident_bf = keep.tile([P, P], BF16)
        make_identity(nc, ident_bf[:])
        ones = keep.tile([P, P], BF16)
        nc.vector.memset(ones[:], 1.0)
        dev_sum = keep.tile([P, FILTERS], F32)
        nc.vector.memset(dev_sum[:], 0.0)
        sq_sum = keep.tile([P, FILTERS], F32)
        nc.vector.memset(sq_sum[:], PIXELS * EPS)
        one = keep.tile([P, 1], F32)
        nc.vector.memset(one[:], 1.0)
        warm = keep.tile([P, 1], F32)
        nc.scalar.activation(out=warm[:], in_=one[:], func=ACT.Abs_reciprocal_sqrt)

        latents_t_ps = banks.tile([P, LATENT // P, P], BF16, tag="bank")
        for c in range(LATENT // P):
            nc.tensor.transpose(latents_t_ps[:, c, :], latents[:, c * P : (c + 1) * P], ident_bf[:])
        latents_t = keep.tile([P, LATENT // P, P], BF16)
        nc.vector.tensor_copy(out=latents_t[:], in_=latents_t_ps[:])

        spread_ps = banks.tile([P, 4 * FILTERS], F32, tag="bank")
        nc.tensor.matmul(
            out=spread_ps[:, 0 : 2 * FILTERS],
            lhsT=ones[:],
            rhs=rows[:, 0 : 2 * FILTERS],
            start=True,
            stop=True,
        )
        for c in range(LATENT // P):
            nc.tensor.matmul(
                out=spread_ps[:, 2 * FILTERS : 4 * FILTERS],
                lhsT=latents_t[:, c, :],
                rhs=dense[:, c, :],
                start=(c == 0),
                stop=False,
            )
        nc.tensor.matmul(
            out=spread_ps[:, 2 * FILTERS : 4 * FILTERS],
            lhsT=ones[:],
            rhs=rows[:, 2 * FILTERS : 4 * FILTERS],
            start=False,
            stop=True,
        )
        per_channel = keep.tile([P, 2 * FILTERS], F32)
        nc.vector.tensor_copy(out=per_channel[:], in_=spread_ps[:, 0 : 2 * FILTERS])
        gamma1 = keep.tile([P, FILTERS], F32)
        nc.vector.tensor_scalar_add(
            out=gamma1[:], in0=spread_ps[:, 2 * FILTERS : 3 * FILTERS], scalar1=1.0
        )
        beta = keep.tile([P, FILTERS], F32)
        nc.vector.tensor_copy(out=beta[:], in_=spread_ps[:, 3 * FILTERS : 4 * FILTERS])

        noise = keep.tile([P, PIXELS], F32)
        nc.vector.tensor_copy(out=noise[:], in_=noise_bf[:])
        noise_bias = keep.tile([P, PIXELS, FILTERS], F32)
        for pixel in range(PIXELS):
            nc.vector.scalar_tensor_tensor(
                out=noise_bias[:, pixel, :],
                in0=per_channel[:, 0:FILTERS],
                scalar=noise[:, pixel : pixel + 1],
                in1=per_channel[:, FILTERS : 2 * FILTERS],
                op0=ALU.mult,
                op1=ALU.add,
            )

        w_grouped = keep.tile([P, PASSES, FILTERS, PACK], BF16, align_bytes=64)
        w_codes = keep.tile([P, PASSES * FILTERS], U32, align_bytes=64)
        w_scales = keep.tile([P, PASSES * FILTERS], U8, align_bytes=64)
        for piece in range(W_PIECES):
            passes = slice(piece * W_PIECE_PASSES, (piece + 1) * W_PIECE_PASSES)
            regroup = nc.scalar.copy if piece % 2 == 0 else nc.vector.tensor_copy
            regroup(
                out=w_grouped[:, passes, :, :],
                in_=w_raw[:, passes, :, :].rearrange("p c t n -> p c n t"),
            )
        for piece in range(W_PIECES):
            passes = slice(piece * W_PIECE_PASSES, (piece + 1) * W_PIECE_PASSES)
            cols = slice(piece * W_PIECE_PASSES * FILTERS, (piece + 1) * W_PIECE_PASSES * FILTERS)
            nc.vector.quantize_mx(
                out=w_codes[:, cols].bitcast(FP8X4),
                scales=w_scales[:, cols],
                in_=w_grouped[:, passes, :, :].rearrange("p c n t -> p (c n t)"),
            )

        def transpose(i):
            if i >= n_chunks:
                return
            passes = chunks[i][2]
            words = x_chunks[i][:].bitcast(F32)
            grouped = grouped_pool.tile([P, CHUNK_COLS], BF16, align_bytes=64, name="grouped")
            grouped_words = grouped[:].bitcast(F32).rearrange("p (g r u) -> p g r u", r=P, u=2)
            for bank in range(passes // BANK_PASSES):
                xt = banks.tile([P, BANK_PASSES, 2, P], F32, tag="bank", name="xt")
                for g in range(BANK_PASSES):
                    for u in range(2):
                        first = ((bank * BANK_PASSES + g) * 2 + u) * P
                        nc.tensor.transpose(xt[:, g, u, :], words[:, first : first + P], ident_f32[:])
                empty = nc.vector.tensor_copy if bank == 3 else nc.scalar.copy
                empty(
                    out=grouped_words[:, bank * BANK_PASSES : (bank + 1) * BANK_PASSES, :, :],
                    in_=xt[:].rearrange("p g u r -> p g r u"),
                )
            grouped_tiles[i] = grouped

        def quantise(i):
            if i < 0 or i >= n_chunks:
                return
            passes = chunks[i][2]
            codes = codes_pool.tile([P, CHUNK_PASSES * P], U32, align_bytes=64, name="codes")
            scales = codes_pool.tile([P, CHUNK_PASSES * P], U8, align_bytes=64, name="scales")
            nc.vector.quantize_mx(
                out=codes[:, : passes * P].bitcast(FP8X4),
                scales=scales[:, : passes * P],
                in_=grouped_tiles[i][:, : passes * K_PASS],
            )
            code_tiles[i] = codes
            scale_tiles[i] = scales

        def multiply(i):
            if i < 0 or i >= n_chunks:
                return
            pixel, first, passes = chunks[i]
            if first == 0:
                conv_sums[pixel] = sums.tile([P, FILTERS], F32, name="conv_sum")
            for g in range(passes):
                c = first + g
                nc.tensor.matmul_mx(
                    out=conv_sums[pixel][:],
                    lhsT=code_tiles[i][:, g * P : (g + 1) * P].bitcast(FP8X4),
                    lhsT_scale=scale_tiles[i][:, g * P : (g + 1) * P],
                    rhs=w_codes[:, c * FILTERS : (c + 1) * FILTERS].bitcast(FP8X4),
                    rhs_scale=w_scales[:, c * FILTERS : (c + 1) * FILTERS],
                    start=(c == 0),
                    stop=(c == PASSES - 1),
                )

        def closes_pixel(i):
            return 0 <= i < n_chunks and chunks[i][1] + chunks[i][2] == PASSES

        relu = keep.tile([P, PIXELS, FILTERS], F32)
        dev = keep.tile([P, PIXELS, FILTERS], F32)

        def add_noise(i):
            if not closes_pixel(i):
                return
            pixel = chunks[i][0]
            pre_relu[pixel] = work.tile([P, FILTERS], F32, name="pre")
            nc.vector.tensor_tensor(
                out=pre_relu[pixel][:],
                in0=conv_sums[pixel][:],
                in1=noise_bias[:, pixel, :],
                op=ALU.add,
            )

        def leaky_relu(i):
            if not closes_pixel(i):
                return
            pixel = chunks[i][0]
            nc.vector.scalar_tensor_tensor(
                out=relu[:, pixel, :],
                in0=pre_relu[pixel][:],
                scalar=SLOPE,
                in1=pre_relu[pixel][:],
                op0=ALU.mult,
                op1=ALU.max,
            )
            nc.gpsimd.tensor_tensor(
                out=dev[:, pixel, :], in0=relu[:, pixel, :], in1=relu[:, 0, :], op=ALU.subtract
            )
            nc.gpsimd.tensor_tensor(
                out=dev_sum[:], in0=dev_sum[:], in1=dev[:, pixel, :], op=ALU.add
            )

        def square(i):
            if not closes_pixel(i):
                return
            pixel = chunks[i][0]
            squares[pixel] = work.tile([P, FILTERS], F32, name="sq")
            nc.scalar.activation(out=squares[pixel][:], in_=dev[:, pixel, :], func=ACT.Square)
            nc.gpsimd.tensor_tensor(out=sq_sum[:], in0=sq_sum[:], in1=squares[pixel][:], op=ALU.add)

        for step in range(n_chunks + 3):
            add_noise(step - 3)
            quantise(step - 1)
            leaky_relu(step - 3)
            transpose(step)
            load(step + X_BUFS)
            if step % 2 == 1:
                multiply(step - 3)
                multiply(step - 2)
            square(step - 3)

        minus_mean_sq = keep.tile([P, FILTERS], F32)
        nc.vector.scalar_tensor_tensor(
            out=minus_mean_sq[:],
            in0=dev_sum[:],
            scalar=-1.0 / (PIXELS * PIXELS),
            in1=dev_sum[:],
            op0=ALU.mult,
            op1=ALU.mult,
        )
        var_eps = keep.tile([P, FILTERS], F32)
        nc.vector.scalar_tensor_tensor(
            out=var_eps[:],
            in0=sq_sum[:],
            scalar=1.0 / PIXELS,
            in1=minus_mean_sq[:],
            op0=ALU.mult,
            op1=ALU.add,
        )
        inv_std = keep.tile([P, FILTERS], F32)
        nc.scalar.activation(out=inv_std[:], in_=var_eps[:], func=ACT.Abs_reciprocal_sqrt)
        gain = keep.tile([P, FILTERS], F32)
        nc.vector.tensor_mul(out=gain[:], in0=inv_std[:], in1=gamma1[:])

        result = keep.tile([P, PIXELS, FILTERS], F32)
        STORE_PIXELS = 4
        for first in range(0, PIXELS, STORE_PIXELS):
            some = slice(first, first + STORE_PIXELS)
            nc.vector.tensor_tensor(
                out=result[:, some, :],
                in0=dev[:, some, :],
                in1=gain[:].unsqueeze(1).to_broadcast([P, STORE_PIXELS, FILTERS]),
                op=ALU.mult,
            )
        mean_gain = keep.tile([P, FILTERS], F32)
        nc.vector.scalar_tensor_tensor(
            out=mean_gain[:],
            in0=dev_sum[:],
            scalar=1.0 / PIXELS,
            in1=gain[:],
            op0=ALU.mult,
            op1=ALU.mult,
        )
        shift = keep.tile([P, FILTERS], F32)
        nc.vector.tensor_sub(out=shift[:], in0=beta[:], in1=mean_gain[:])
        for first in range(0, PIXELS, STORE_PIXELS):
            some = slice(first, first + STORE_PIXELS)
            nc.vector.tensor_tensor(
                out=result[:, some, :],
                in0=result[:, some, :],
                in1=shift[:].unsqueeze(1).to_broadcast([P, STORE_PIXELS, FILTERS]),
                op=ALU.add,
            )
            nc.sync.dma_start(out=out_rows[:, some, :], in_=result[:, some, :])
